import numpy as np
import ml_dtypes


def mxq(x, axis, fmt="e4m3"):
    dtype, down = {"e4m3": (ml_dtypes.float8_e4m3fn, 7), "e5m2": (ml_dtypes.float8_e5m2, 14)}[fmt]
    v = np.moveaxis(np.asarray(x, np.float32).astype(ml_dtypes.bfloat16).astype(np.float64), axis, -1)
    blocks = v.reshape(v.shape[:-1] + (-1, 32))
    amax = np.abs(blocks).max(-1, keepdims=True)
    byte = np.maximum(np.where(amax > 0, np.frexp(amax)[1] - 1 + 127, 0) - down, 1)
    scale = np.exp2(byte - 127.0)
    codes = (blocks / scale).astype(np.float32).astype(dtype).astype(np.float64)
    return np.moveaxis((codes * scale).reshape(v.shape), -1, axis)


WIDE = False


def mx_kscale(k):
    if not WIDE:
        return np.ones(k)
    levels = np.array([10, -10, 5, -5, 0])
    if k % 512:
        return np.exp2(np.random.permutation(np.resize(levels, k // 32))).repeat(32)
    a = np.empty((k // 512, 16))
    for p in range(k // 512):
        a[p, :8] = np.random.permutation(np.resize(levels, 8))
        for g in range(8):
            far = levels[np.abs(levels - a[p, g]) >= 10]
            a[p, g + 8] = far[np.random.randint(len(far))]
    return np.exp2(a.ravel()).repeat(32)


BF16 = ml_dtypes.bfloat16


def bf(x):
    return np.asarray(x, np.float32).astype(BF16)


def f64(x):
    return np.asarray(x).astype(np.float64)


N, LMAX, CIN, COUT = 512, 3, 1024, 128
NL = LMAX + 1
NM = NL * NL


def setup_inputs():
    s = mx_kscale(CIN)
    return {"x": bf(np.random.standard_normal((N, NM, CIN)) * s),
            "weights": bf(np.random.standard_normal((NL, CIN, COUT)) / np.sqrt(CIN) / s[:, None]),
            "path_weights": bf(1.0 + 0.3 * np.random.standard_normal(NL))}


def reference(x, weights, path_weights):
    x, weights, path_weights = f64(x), f64(weights), f64(path_weights)
    blocks = []
    for l in range(LMAX + 1):
        start = l * l
        end = start + (2 * l + 1)
        blk = mxq(x[:, start:end, :], 2, "e4m3") @ mxq(weights[l], 0, "e4m3")
        blocks.append(path_weights[l] * blk)
    return np.concatenate(blocks, axis=1)

@@ -1,0 +1,165 @@
+import concourse.mybir as mybir
+from concourse.masks import make_identity
+
+BF16 = mybir.dt.bfloat16
+F32 = mybir.dt.float32
+U32 = mybir.dt.uint32
+U8 = mybir.dt.uint8
+FP8X4 = mybir.dt.float8_e4m3fn_x4
+
+NODES, ROWS, CIN, COUT, DEGREES = 512, 16, 1024, 128, 4
+FLOPS = 2 * NODES * ROWS * CIN * COUT
+
+P = 128
+PACK = 4
+K_PASS = P * PACK
+PASSES = CIN // K_PASS
+WORDS = CIN // 2
+HALVES = PACK // 2
+
+DEGREE_OF_ROW = [l for l in range(DEGREES) for i in range(2 * l + 1)]
+
+UNITS = 4
+ROUNDS_PER_NODE_TILE = ROWS // UNITS
+ROUNDS = (NODES // P) * ROUNDS_PER_NODE_TILE
+
+
+def tile_linear_pa_t_kernel(tc, x, weights, path_weights, out):
+    nc = tc.nc
+    with (
+        tc.tile_pool(name="const", bufs=1) as const,
+        tc.tile_pool(name="x_pool", bufs=ROUNDS) as x_pool,
+        tc.tile_pool(name="grouped_pool", bufs=3) as grouped_pool,
+        tc.tile_pool(name="quantised_pool", bufs=3) as quantised_pool,
+        tc.tile_pool(name="out_pool", bufs=NODES // P) as out_pool,
+        tc.psum_pool(name="xt_pool", bufs=6) as xt_pool,
+        tc.psum_pool(name="acc_pool", bufs=2) as acc_pool,
+        tc.manual_schedule(),
+    ):
+        def load_x_round(r):
+            n0 = (r // ROUNDS_PER_NODE_TILE) * P
+            m0 = (r % ROUNDS_PER_NODE_TILE) * UNITS
+            x_sb = x_pool.tile([P, UNITS * CIN], BF16)
+            nc.sync.dma_start(
+                out=x_sb[:], in_=x[n0 : n0 + P, m0 : m0 + UNITS, :].rearrange("n m k -> n (m k)")
+            )
+            return x_sb
+
+        x_tiles = [load_x_round(0)]
+
+        w_raw = const.tile([P, DEGREES * CIN], BF16)
+        for l in range(DEGREES):
+            nc.sync.dma_start(
+                out=w_raw[:, l * CIN : (l + 1) * CIN].rearrange("p (g tc) -> p g tc", tc=PACK * COUT),
+                in_=weights[l].rearrange("(g p t) c -> p g (t c)", p=P, t=PACK),
+            )
+        pw_bf16 = const.tile([P, DEGREES], BF16)
+        nc.scalar.dma_start(out=pw_bf16[:], in_=path_weights.partition_broadcast(P))
+
+        for r in range(1, ROUNDS):
+            x_tiles.append(load_x_round(r))
+
+        ident = const.tile([P, P], F32)
+        make_identity(nc, ident[:])
+        pw = const.tile([P, DEGREES], F32)
+        nc.vector.tensor_copy(out=pw[:], in_=pw_bf16[:])
+
+        w_grouped = const.tile([P, DEGREES * CIN], BF16, align_bytes=64)
+        for l in range(DEGREES):
+            nc.vector.tensor_copy(
+                out=w_grouped[:, l * CIN : (l + 1) * CIN].rearrange("p (g c t) -> p g c t", c=COUT, t=PACK),
+                in_=w_raw[:, l * CIN : (l + 1) * CIN].rearrange("p (g t c) -> p g c t", c=COUT, t=PACK),
+            )
+        w_codes = const.tile([P, DEGREES * PASSES * COUT], U32, align_bytes=64)
+        w_scales = const.tile([P, DEGREES * PASSES * COUT], U8, align_bytes=64)
+        nc.vector.quantize_mx(out=w_codes[:].bitcast(FP8X4), scales=w_scales[:], in_=w_grouped[:])
+
+        def transpose_round(r):
+            x_words = x_tiles[r][:].bitcast(F32)
+            grouped = grouped_pool.tile([P, UNITS * CIN], BF16, align_bytes=64)
+            for unit in range(UNITS):
+                xt = xt_pool.tile([P, WORDS], F32)
+                for j in range(WORDS // P):
+                    g, u = divmod(j, HALVES)
+                    first = unit * WORDS + g * HALVES * P + u
+                    last = first + HALVES * (P - 1)
+                    nc.tensor.transpose(
+                        xt[:, j * P : (j + 1) * P],
+                        x_words[:, first : last + 1 : HALVES],
+                        ident[:],
+                    )
+                copy = nc.vector.tensor_copy if unit == 0 else nc.scalar.copy
+                copy(
+                    out=grouped[:, unit * CIN : (unit + 1) * CIN]
+                    .bitcast(F32)
+                    .rearrange("p (g n u) -> p g n u", g=PASSES, u=HALVES),
+                    in_=xt[:].rearrange("p (g u n) -> p g n u", g=PASSES, u=HALVES),
+                )
+            return grouped
+
+        def quantise_round(grouped):
+            codes = quantised_pool.tile([P, UNITS * PASSES * P], U32, align_bytes=64)
+            scales = quantised_pool.tile([P, UNITS * PASSES * P], U8, align_bytes=64)
+            nc.vector.quantize_mx(out=codes[:].bitcast(FP8X4), scales=scales[:], in_=grouped[:])
+            return codes, scales
+
+        def multiply_round(r, codes, scales, out_sb):
+            m0 = (r % ROUNDS_PER_NODE_TILE) * UNITS
+            acc = acc_pool.tile([P, UNITS * COUT], F32)
+            for unit in range(UNITS):
+                l = DEGREE_OF_ROW[m0 + unit]
+                for g in range(PASSES):
+                    x_cols = slice((unit * PASSES + g) * P, (unit * PASSES + g + 1) * P)
+                    w_cols = slice((l * PASSES + g) * COUT, (l * PASSES + g + 1) * COUT)
+                    nc.tensor.matmul_mx(
+                        out=acc[:, unit * COUT : (unit + 1) * COUT],
+                        lhsT=codes[:, x_cols].bitcast(FP8X4),
+                        lhsT_scale=scales[:, x_cols],
+                        rhs=w_codes[:, w_cols].bitcast(FP8X4),
+                        rhs_scale=w_scales[:, w_cols],
+                        start=(g == 0),
+                        stop=(g == PASSES - 1),
+                    )
+            for l in range(DEGREES):
+                units_of_l = [unit for unit in range(UNITS) if DEGREE_OF_ROW[m0 + unit] == l]
+                if not units_of_l:
+                    continue
+                first, count = units_of_l[0], len(units_of_l)
+                src = acc[:, first * COUT : (first + count) * COUT]
+                dst = out_sb[:, (m0 + first) * COUT : (m0 + first + count) * COUT]
+                if r % 2 == 0:
+                    nc.vector.tensor_scalar(
+                        out=dst, in0=src, scalar1=pw[:, l : l + 1], scalar2=None, op0=mybir.AluOpType.mult
+                    )
+                else:
+                    nc.scalar.activation(
+                        out=dst, in_=src, func=mybir.ActivationFunctionType.Copy, scale=pw[:, l : l + 1]
+                    )
+
+        def store_rows(r, out_sb, first_row, rows):
+            n0 = (r // ROUNDS_PER_NODE_TILE) * P
+            nc.sync.dma_start(
+                out=out[n0 : n0 + P, first_row : first_row + rows, :].rearrange("n m c -> n (m c)"),
+                in_=out_sb[:, first_row * COUT : (first_row + rows) * COUT],
+            )
+
+        grouped_of = {}
+        quantised_of = {}
+        out_of = {}
+        for s in range(ROUNDS + 2):
+            if s < ROUNDS:
+                grouped_of[s] = transpose_round(s)
+            if 1 <= s <= ROUNDS:
+                quantised_of[s - 1] = quantise_round(grouped_of[s - 1])
+            if s >= 2:
+                r = s - 2
+                node_tile = r // ROUNDS_PER_NODE_TILE
+                if r % ROUNDS_PER_NODE_TILE == 0:
+                    out_sb = out_pool.tile([P, ROWS * COUT], F32)
+                    out_of[node_tile] = out_sb
+                codes, scales = quantised_of[r]
+                multiply_round(r, codes, scales, out_of[node_tile])
+                if node_tile == NODES // P - 1:
+                    store_rows(r, out_of[node_tile], (r % ROUNDS_PER_NODE_TILE) * UNITS, UNITS)
+                elif r % ROUNDS_PER_NODE_TILE == ROUNDS_PER_NODE_TILE - 1:
+                    store_rows(r, out_of[node_tile], 0, ROWS)

@@ -23,12 +23,15 @@ UNITS = 4
 ROUNDS_PER_NODE_TILE = ROWS // UNITS
 ROUNDS = (NODES // P) * ROUNDS_PER_NODE_TILE
 
+ORDERED = 2
+
 
 def tile_linear_pa_t_kernel(tc, x, weights, path_weights, out):
     nc = tc.nc
     with (
         tc.tile_pool(name="const", bufs=1) as const,
         tc.tile_pool(name="x_pool", bufs=ROUNDS) as x_pool,
+        tc.tile_pool(name="ordered_pool", bufs=3) as ordered_pool,
         tc.tile_pool(name="grouped_pool", bufs=3) as grouped_pool,
         tc.tile_pool(name="quantised_pool", bufs=3) as quantised_pool,
         tc.tile_pool(name="out_pool", bufs=NODES // P) as out_pool,
@@ -53,16 +56,29 @@ def tile_linear_pa_t_kernel(tc, x, weights, path_weights, out):
                 out=w_raw[:, l * CIN : (l + 1) * CIN].rearrange("p (g tc) -> p g tc", tc=PACK * COUT),
                 in_=weights[l].rearrange("(g p t) c -> p g (t c)", p=P, t=PACK),
             )
-        pw_bf16 = const.tile([P, DEGREES], BF16)
-        nc.scalar.dma_start(out=pw_bf16[:], in_=path_weights.partition_broadcast(P))
+        pw_row = const.tile([P, DEGREES], BF16)
+        nc.gpsimd.memset(pw_row[:], 0.0)
+        nc.scalar.dma_start(out=pw_row[0:1, :], in_=path_weights.rearrange("(o l) -> o l", o=1))
 
         for r in range(1, ROUNDS):
             x_tiles.append(load_x_round(r))
 
         ident = const.tile([P, P], F32)
         make_identity(nc, ident[:])
+        ones = const.tile([P, P], BF16)
+        nc.gpsimd.memset(ones[:], 1.0)
         pw = const.tile([P, DEGREES], F32)
-        nc.vector.tensor_copy(out=pw[:], in_=pw_bf16[:])
+
+        def order_round(r):
+            x_words = x_tiles[r][:].bitcast(F32)
+            ordered = ordered_pool.tile([P, ORDERED * CIN], BF16)
+            nc.vector.tensor_copy(
+                out=ordered[:].bitcast(F32).rearrange("p (b u w) -> p b u w", u=HALVES, w=P),
+                in_=x_words[:, (UNITS - ORDERED) * WORDS :].rearrange("p (b w u) -> p b u w", w=P, u=HALVES),
+            )
+            return ordered
+
+        ordered_of = {0: order_round(0)}
 
         w_grouped = const.tile([P, DEGREES * CIN], BF16, align_bytes=64)
         for l in range(DEGREES):
@@ -74,22 +90,22 @@ def tile_linear_pa_t_kernel(tc, x, weights, path_weights, out):
         w_scales = const.tile([P, DEGREES * PASSES * COUT], U8, align_bytes=64)
         nc.vector.quantize_mx(out=w_codes[:].bitcast(FP8X4), scales=w_scales[:], in_=w_grouped[:])
 
-        def transpose_round(r):
+        def transpose_round(r, ordered):
             x_words = x_tiles[r][:].bitcast(F32)
+            ordered_words = ordered[:].bitcast(F32)
             grouped = grouped_pool.tile([P, UNITS * CIN], BF16, align_bytes=64)
             for unit in range(UNITS):
                 xt = xt_pool.tile([P, WORDS], F32)
                 for j in range(WORDS // P):
                     g, u = divmod(j, HALVES)
-                    first = unit * WORDS + g * HALVES * P + u
-                    last = first + HALVES * (P - 1)
-                    nc.tensor.transpose(
-                        xt[:, j * P : (j + 1) * P],
-                        x_words[:, first : last + 1 : HALVES],
-                        ident[:],
-                    )
-                copy = nc.vector.tensor_copy if unit == 0 else nc.scalar.copy
-                copy(
+                    if unit < UNITS - ORDERED:
+                        first = unit * WORDS + g * HALVES * P + u
+                        words = x_words[:, first : first + HALVES * (P - 1) + 1 : HALVES]
+                    else:
+                        first = (unit - (UNITS - ORDERED)) * WORDS + j * P
+                        words = ordered_words[:, first : first + P]
+                    nc.tensor.transpose(xt[:, j * P : (j + 1) * P], words, ident[:])
+                nc.scalar.copy(
                     out=grouped[:, unit * CIN : (unit + 1) * CIN]
                     .bitcast(F32)
                     .rearrange("p (g n u) -> p g n u", g=PASSES, u=HALVES),
@@ -148,7 +164,11 @@ def tile_linear_pa_t_kernel(tc, x, weights, path_weights, out):
         out_of = {}
         for s in range(ROUNDS + 2):
             if s < ROUNDS:
-                grouped_of[s] = transpose_round(s)
+                grouped_of[s] = transpose_round(s, ordered_of[s])
+            if s == 0:
+                acc = acc_pool.tile([P, UNITS * COUT], F32)
+                nc.tensor.matmul(out=acc[:, :DEGREES], lhsT=ones[:], rhs=pw_row[:], start=True, stop=True)
+                nc.vector.tensor_copy(out=pw[:], in_=acc[:, :DEGREES])
             if 1 <= s <= ROUNDS:
                 quantised_of[s - 1] = quantise_round(grouped_of[s - 1])
             if s >= 2:
@@ -163,3 +183,5 @@ def tile_linear_pa_t_kernel(tc, x, weights, path_weights, out):
                     store_rows(r, out_of[node_tile], (r % ROUNDS_PER_NODE_TILE) * UNITS, UNITS)
                 elif r % ROUNDS_PER_NODE_TILE == ROUNDS_PER_NODE_TILE - 1:
                     store_rows(r, out_of[node_tile], 0, ROWS)
+            if s + 1 < ROUNDS:
+                ordered_of[s + 1] = order_round(s + 1)

@@ -23,15 +23,15 @@ UNITS = 4
 ROUNDS_PER_NODE_TILE = ROWS // UNITS
 ROUNDS = (NODES // P) * ROUNDS_PER_NODE_TILE
 
-ORDERED = 2
+ORDERED = 3
 
 
 def tile_linear_pa_t_kernel(tc, x, weights, path_weights, out):
     nc = tc.nc
     with (
         tc.tile_pool(name="const", bufs=1) as const,
-        tc.tile_pool(name="x_pool", bufs=ROUNDS) as x_pool,
-        tc.tile_pool(name="ordered_pool", bufs=3) as ordered_pool,
+        tc.tile_pool(name="x_pool", bufs=14) as x_pool,
+        tc.tile_pool(name="ordered_pool", bufs=4) as ordered_pool,
         tc.tile_pool(name="grouped_pool", bufs=3) as grouped_pool,
         tc.tile_pool(name="quantised_pool", bufs=3) as quantised_pool,
         tc.tile_pool(name="out_pool", bufs=NODES // P) as out_pool,
@@ -89,6 +89,7 @@ def tile_linear_pa_t_kernel(tc, x, weights, path_weights, out):
         w_codes = const.tile([P, DEGREES * PASSES * COUT], U32, align_bytes=64)
         w_scales = const.tile([P, DEGREES * PASSES * COUT], U8, align_bytes=64)
         nc.vector.quantize_mx(out=w_codes[:].bitcast(FP8X4), scales=w_scales[:], in_=w_grouped[:])
+        ordered_of[1] = order_round(1)
 
         def transpose_round(r, ordered):
             x_words = x_tiles[r][:].bitcast(F32)
@@ -171,6 +172,8 @@ def tile_linear_pa_t_kernel(tc, x, weights, path_weights, out):
                 nc.vector.tensor_copy(out=pw[:], in_=acc[:, :DEGREES])
             if 1 <= s <= ROUNDS:
                 quantised_of[s - 1] = quantise_round(grouped_of[s - 1])
+            if s + 2 < ROUNDS:
+                ordered_of[s + 2] = order_round(s + 2)
             if s >= 2:
                 r = s - 2
                 node_tile = r // ROUNDS_PER_NODE_TILE
@@ -183,5 +186,3 @@ def tile_linear_pa_t_kernel(tc, x, weights, path_weights, out):
                     store_rows(r, out_of[node_tile], (r % ROUNDS_PER_NODE_TILE) * UNITS, UNITS)
                 elif r % ROUNDS_PER_NODE_TILE == ROUNDS_PER_NODE_TILE - 1:
                     store_rows(r, out_of[node_tile], 0, ROWS)
-            if s + 1 < ROUNDS:
-                ordered_of[s + 1] = order_round(s + 1)

@@ -19,12 +19,25 @@ HALVES = PACK // 2
 
 DEGREE_OF_ROW = [l for l in range(DEGREES) for i in range(2 * l + 1)]
 
-UNITS = 4
-ROUNDS_PER_NODE_TILE = ROWS // UNITS
-ROUNDS = (NODES // P) * ROUNDS_PER_NODE_TILE
+NODE_TILES = NODES // P
+MAX_UNITS = 4
+HEAD, BODY, TAIL = [1, 1, 2, 2, 2, 4, 4], [4, 4, 4, 4], [4, 4, 4, 2, 1, 1]
+
+
+def all_rounds():
+    rounds = []
+    for tile in range(NODE_TILES):
+        sizes = HEAD if tile == 0 else TAIL if tile == NODE_TILES - 1 else BODY
+        first_row = 0
+        for units in sizes:
+            rounds.append((tile, first_row, units))
+            first_row += units
+    return rounds
+
 
 ORDERED = 3
 
+X_BUFS = {1: 4, 2: 4, 4: 11}
 
 def tile_linear_pa_t_kernel(tc, x, weights, path_weights, out):
     nc = tc.nc
@@ -34,34 +47,43 @@ def tile_linear_pa_t_kernel(tc, x, weights, path_weights, out):
         tc.tile_pool(name="ordered_pool", bufs=4) as ordered_pool,
         tc.tile_pool(name="grouped_pool", bufs=3) as grouped_pool,
         tc.tile_pool(name="quantised_pool", bufs=3) as quantised_pool,
-        tc.tile_pool(name="out_pool", bufs=NODES // P) as out_pool,
+        tc.tile_pool(name="out_pool", bufs=NODE_TILES) as out_pool,
         tc.psum_pool(name="xt_pool", bufs=6) as xt_pool,
         tc.psum_pool(name="acc_pool", bufs=2) as acc_pool,
         tc.manual_schedule(),
     ):
+        rounds = all_rounds()
+
         def load_x_round(r):
-            n0 = (r // ROUNDS_PER_NODE_TILE) * P
-            m0 = (r % ROUNDS_PER_NODE_TILE) * UNITS
-            x_sb = x_pool.tile([P, UNITS * CIN], BF16)
+            tile, first_row, units = rounds[r]
+            x_sb = x_pool.tile([P, units * CIN], BF16, tag=f"x{units}", bufs=X_BUFS[units])
             nc.sync.dma_start(
-                out=x_sb[:], in_=x[n0 : n0 + P, m0 : m0 + UNITS, :].rearrange("n m k -> n (m k)")
+                out=x_sb[:],
+                in_=x[tile * P : (tile + 1) * P, first_row : first_row + units, :].rearrange("n m k -> n (m k)"),
             )
             return x_sb
 
-        x_tiles = [load_x_round(0)]
-
         w_raw = const.tile([P, DEGREES * CIN], BF16)
-        for l in range(DEGREES):
+
+        def load_weights(l):
             nc.sync.dma_start(
                 out=w_raw[:, l * CIN : (l + 1) * CIN].rearrange("p (g tc) -> p g tc", tc=PACK * COUT),
                 in_=weights[l].rearrange("(g p t) c -> p g (t c)", p=P, t=PACK),
             )
+
+        x_tiles = [load_x_round(0), load_x_round(1)]
+        load_weights(0)
+        load_weights(1)
+        for r in range(2, 5):
+            x_tiles.append(load_x_round(r))
+        load_weights(2)
+        load_weights(3)
+        for r in range(5, len(rounds)):
+            x_tiles.append(load_x_round(r))
+
         pw_row = const.tile([P, DEGREES], BF16)
         nc.gpsimd.memset(pw_row[:], 0.0)
         nc.scalar.dma_start(out=pw_row[0:1, :], in_=path_weights.rearrange("(o l) -> o l", o=1))
-
-        for r in range(1, ROUNDS):
-            x_tiles.append(load_x_round(r))
 
         ident = const.tile([P, P], F32)
         make_identity(nc, ident[:])
@@ -69,42 +91,49 @@ def tile_linear_pa_t_kernel(tc, x, weights, path_weights, out):
         nc.gpsimd.memset(ones[:], 1.0)
         pw = const.tile([P, DEGREES], F32)
 
-        def order_round(r):
-            x_words = x_tiles[r][:].bitcast(F32)
-            ordered = ordered_pool.tile([P, ORDERED * CIN], BF16)
-            nc.vector.tensor_copy(
-                out=ordered[:].bitcast(F32).rearrange("p (b u w) -> p b u w", u=HALVES, w=P),
-                in_=x_words[:, (UNITS - ORDERED) * WORDS :].rearrange("p (b w u) -> p b u w", w=P, u=HALVES),
-            )
-            return ordered
-
-        ordered_of = {0: order_round(0)}
-
         w_grouped = const.tile([P, DEGREES * CIN], BF16, align_bytes=64)
-        for l in range(DEGREES):
+        w_codes = const.tile([P, DEGREES * PASSES * COUT], U32, align_bytes=64)
+        w_scales = const.tile([P, DEGREES * PASSES * COUT], U8, align_bytes=64)
+
+        def group_weights(l):
             nc.vector.tensor_copy(
                 out=w_grouped[:, l * CIN : (l + 1) * CIN].rearrange("p (g c t) -> p g c t", c=COUT, t=PACK),
                 in_=w_raw[:, l * CIN : (l + 1) * CIN].rearrange("p (g t c) -> p g c t", c=COUT, t=PACK),
             )
-        w_codes = const.tile([P, DEGREES * PASSES * COUT], U32, align_bytes=64)
-        w_scales = const.tile([P, DEGREES * PASSES * COUT], U8, align_bytes=64)
-        nc.vector.quantize_mx(out=w_codes[:].bitcast(FP8X4), scales=w_scales[:], in_=w_grouped[:])
-        ordered_of[1] = order_round(1)
+
+        def quantise_weights(first, count):
+            words = slice(first * PASSES * COUT, (first + count) * PASSES * COUT)
+            nc.vector.quantize_mx(
+                out=w_codes[:, words].bitcast(FP8X4),
+                scales=w_scales[:, words],
+                in_=w_grouped[:, first * CIN : (first + count) * CIN],
+            )
+
+        def order_round(r):
+            if rounds[r][2] < MAX_UNITS:
+                return None
+            x_words = x_tiles[r][:].bitcast(F32)
+            ordered = ordered_pool.tile([P, ORDERED * CIN], BF16)
+            nc.vector.tensor_copy(
+                out=ordered[:].bitcast(F32).rearrange("p (b u w) -> p b u w", u=HALVES, w=P),
+                in_=x_words[:, (MAX_UNITS - ORDERED) * WORDS :].rearrange("p (b w u) -> p b u w", w=P, u=HALVES),
+            )
+            return ordered
 
         def transpose_round(r, ordered):
+            units = rounds[r][2]
             x_words = x_tiles[r][:].bitcast(F32)
-            ordered_words = ordered[:].bitcast(F32)
-            grouped = grouped_pool.tile([P, UNITS * CIN], BF16, align_bytes=64)
-            for unit in range(UNITS):
+            grouped = grouped_pool.tile([P, units * CIN], BF16, tag="grouped", align_bytes=64)
+            for unit in range(units):
                 xt = xt_pool.tile([P, WORDS], F32)
                 for j in range(WORDS // P):
                     g, u = divmod(j, HALVES)
-                    if unit < UNITS - ORDERED:
+                    if ordered is None or unit < MAX_UNITS - ORDERED:
                         first = unit * WORDS + g * HALVES * P + u
                         words = x_words[:, first : first + HALVES * (P - 1) + 1 : HALVES]
                     else:
-                        first = (unit - (UNITS - ORDERED)) * WORDS + j * P
-                        words = ordered_words[:, first : first + P]
+                        first = (unit - (MAX_UNITS - ORDERED)) * WORDS + j * P
+                        words = ordered[:].bitcast(F32)[:, first : first + P]
                     nc.tensor.transpose(xt[:, j * P : (j + 1) * P], words, ident[:])
                 nc.scalar.copy(
                     out=grouped[:, unit * CIN : (unit + 1) * CIN]
@@ -114,17 +143,18 @@ def tile_linear_pa_t_kernel(tc, x, weights, path_weights, out):
                 )
             return grouped
 
-        def quantise_round(grouped):
-            codes = quantised_pool.tile([P, UNITS * PASSES * P], U32, align_bytes=64)
-            scales = quantised_pool.tile([P, UNITS * PASSES * P], U8, align_bytes=64)
+        def quantise_round(r, grouped):
+            words = rounds[r][2] * PASSES * P
+            codes = quantised_pool.tile([P, words], U32, tag="codes", align_bytes=64)
+            scales = quantised_pool.tile([P, words], U8, tag="scales", align_bytes=64)
             nc.vector.quantize_mx(out=codes[:].bitcast(FP8X4), scales=scales[:], in_=grouped[:])
             return codes, scales
 
         def multiply_round(r, codes, scales, out_sb):
-            m0 = (r % ROUNDS_PER_NODE_TILE) * UNITS
-            acc = acc_pool.tile([P, UNITS * COUT], F32)
-            for unit in range(UNITS):
-                l = DEGREE_OF_ROW[m0 + unit]
+            first_row, units = rounds[r][1:]
+            acc = acc_pool.tile([P, MAX_UNITS * COUT], F32)
+            for unit in range(units):
+                l = DEGREE_OF_ROW[first_row + unit]
                 for g in range(PASSES):
                     x_cols = slice((unit * PASSES + g) * P, (unit * PASSES + g + 1) * P)
                     w_cols = slice((l * PASSES + g) * COUT, (l * PASSES + g + 1) * COUT)
@@ -138,12 +168,12 @@ def tile_linear_pa_t_kernel(tc, x, weights, path_weights, out):
                         stop=(g == PASSES - 1),
                     )
             for l in range(DEGREES):
-                units_of_l = [unit for unit in range(UNITS) if DEGREE_OF_ROW[m0 + unit] == l]
+                units_of_l = [unit for unit in range(units) if DEGREE_OF_ROW[first_row + unit] == l]
                 if not units_of_l:
                     continue
                 first, count = units_of_l[0], len(units_of_l)
                 src = acc[:, first * COUT : (first + count) * COUT]
-                dst = out_sb[:, (m0 + first) * COUT : (m0 + first + count) * COUT]
+                dst = out_sb[:, (first_row + first) * COUT : (first_row + first + count) * COUT]
                 if r % 2 == 0:
                     nc.vector.tensor_scalar(
                         out=dst, in0=src, scalar1=pw[:, l : l + 1], scalar2=None, op0=mybir.AluOpType.mult
@@ -153,36 +183,45 @@ def tile_linear_pa_t_kernel(tc, x, weights, path_weights, out):
                         out=dst, in_=src, func=mybir.ActivationFunctionType.Copy, scale=pw[:, l : l + 1]
                     )
 
-        def store_rows(r, out_sb, first_row, rows):
-            n0 = (r // ROUNDS_PER_NODE_TILE) * P
+        def store_rows(tile, out_sb, first_row, rows):
             nc.sync.dma_start(
-                out=out[n0 : n0 + P, first_row : first_row + rows, :].rearrange("n m c -> n (m c)"),
+                out=out[tile * P : (tile + 1) * P, first_row : first_row + rows, :].rearrange("n m c -> n (m c)"),
                 in_=out_sb[:, first_row * COUT : (first_row + rows) * COUT],
             )
 
+        ordered_of = {}
         grouped_of = {}
         quantised_of = {}
         out_of = {}
-        for s in range(ROUNDS + 2):
-            if s < ROUNDS:
+        for r in range(2):
+            ordered_of[r] = order_round(r)
+        for s in range(len(rounds) + 2):
+            if s < len(rounds):
                 grouped_of[s] = transpose_round(s, ordered_of[s])
             if s == 0:
-                acc = acc_pool.tile([P, UNITS * COUT], F32)
+                for l in (0, 1):
+                    group_weights(l)
+                quantise_weights(0, 2)
+                acc = acc_pool.tile([P, MAX_UNITS * COUT], F32)
                 nc.tensor.matmul(out=acc[:, :DEGREES], lhsT=ones[:], rhs=pw_row[:], start=True, stop=True)
                 nc.vector.tensor_copy(out=pw[:], in_=acc[:, :DEGREES])
-            if 1 <= s <= ROUNDS:
-                quantised_of[s - 1] = quantise_round(grouped_of[s - 1])
-            if s + 2 < ROUNDS:
+            if 1 <= s <= len(rounds):
+                quantised_of[s - 1] = quantise_round(s - 1, grouped_of[s - 1])
+            if s == 3:
+                for l in (2, 3):
+                    group_weights(l)
+                quantise_weights(2, 2)
+            if s + 2 < len(rounds):
                 ordered_of[s + 2] = order_round(s + 2)
             if s >= 2:
                 r = s - 2
-                node_tile = r // ROUNDS_PER_NODE_TILE
-                if r % ROUNDS_PER_NODE_TILE == 0:
+                tile, first_row, units = rounds[r]
+                if first_row == 0:
                     out_sb = out_pool.tile([P, ROWS * COUT], F32)
-                    out_of[node_tile] = out_sb
+                    out_of[tile] = out_sb
                 codes, scales = quantised_of[r]
-                multiply_round(r, codes, scales, out_of[node_tile])
-                if node_tile == NODES // P - 1:
-                    store_rows(r, out_of[node_tile], (r % ROUNDS_PER_NODE_TILE) * UNITS, UNITS)
-                elif r % ROUNDS_PER_NODE_TILE == ROUNDS_PER_NODE_TILE - 1:
-                    store_rows(r, out_of[node_tile], 0, ROWS)
+                multiply_round(r, codes, scales, out_of[tile])
+                if tile == NODE_TILES - 1:
+                    store_rows(tile, out_of[tile], first_row, units)
+                elif first_row + units == ROWS:
+                    store_rows(tile, out_of[tile], 0, ROWS)

@@ -35,9 +35,9 @@ def all_rounds():
     return rounds
 
 
-ORDERED = 3
+ORDERED = 2
 
-X_BUFS = {1: 4, 2: 4, 4: 11}
+X_BUFS = {1: 4, 2: 4, 4: 12}
 
 def tile_linear_pa_t_kernel(tc, x, weights, path_weights, out):
     nc = tc.nc

@@ -21,18 +21,24 @@ DEGREE_OF_ROW = [l for l in range(DEGREES) for i in range(2 * l + 1)]
 
 NODE_TILES = NODES // P
 MAX_UNITS = 4
-HEAD, BODY, TAIL = [1, 1, 2, 2, 2, 4, 4], [4, 4, 4, 4], [4, 4, 4, 2, 1, 1]
+HEAD = [(9, 1), (10, 2), (12, 2), (0, 1), (14, 2), (5, 4), (1, 4)]
+BODY = [(0, 4), (4, 4), (8, 4), (12, 4)]
+TAIL = [(0, 4), (4, 4), (8, 4), (12, 2), (14, 1), (15, 1)]
 
 
 def all_rounds():
     rounds = []
     for tile in range(NODE_TILES):
-        sizes = HEAD if tile == 0 else TAIL if tile == NODE_TILES - 1 else BODY
-        first_row = 0
-        for units in sizes:
-            rounds.append((tile, first_row, units))
-            first_row += units
+        of_tile = HEAD if tile == 0 else TAIL if tile == NODE_TILES - 1 else BODY
+        rounds.extend([(tile, first_row, units) for first_row, units in of_tile])
     return rounds
+
+
+def new_degrees(rounds, r):
+    tile, first_row, units = rounds[r]
+    degrees = sorted(set(DEGREE_OF_ROW[first_row : first_row + units]))
+    earlier = [DEGREE_OF_ROW[row] for t, first, count in rounds[:r] for row in range(first, first + count)]
+    return [l for l in degrees if l not in earlier]
 
 
 ORDERED = 2
@@ -71,15 +77,11 @@ def tile_linear_pa_t_kernel(tc, x, weights, path_weights, out):
                 in_=weights[l].rearrange("(g p t) c -> p g (t c)", p=P, t=PACK),
             )
 
-        x_tiles = [load_x_round(0), load_x_round(1)]
-        load_weights(0)
-        load_weights(1)
-        for r in range(2, 5):
+        x_tiles = []
+        for r in range(len(rounds)):
             x_tiles.append(load_x_round(r))
-        load_weights(2)
-        load_weights(3)
-        for r in range(5, len(rounds)):
-            x_tiles.append(load_x_round(r))
+            for l in new_degrees(rounds, r):
+                load_weights(l)
 
         pw_row = const.tile([P, DEGREES], BF16)
         nc.gpsimd.memset(pw_row[:], 0.0)
@@ -101,12 +103,12 @@ def tile_linear_pa_t_kernel(tc, x, weights, path_weights, out):
                 in_=w_raw[:, l * CIN : (l + 1) * CIN].rearrange("p (g t c) -> p g c t", c=COUT, t=PACK),
             )
 
-        def quantise_weights(first, count):
-            words = slice(first * PASSES * COUT, (first + count) * PASSES * COUT)
+        def quantise_weights(l):
+            words = slice(l * PASSES * COUT, (l + 1) * PASSES * COUT)
             nc.vector.quantize_mx(
                 out=w_codes[:, words].bitcast(FP8X4),
                 scales=w_scales[:, words],
-                in_=w_grouped[:, first * CIN : (first + count) * CIN],
+                in_=w_grouped[:, l * CIN : (l + 1) * CIN],
             )
 
         def order_round(r):
@@ -193,35 +195,31 @@ def tile_linear_pa_t_kernel(tc, x, weights, path_weights, out):
         grouped_of = {}
         quantised_of = {}
         out_of = {}
-        for r in range(2):
-            ordered_of[r] = order_round(r)
+        ordered_of[0] = order_round(0)
         for s in range(len(rounds) + 2):
             if s < len(rounds):
                 grouped_of[s] = transpose_round(s, ordered_of[s])
             if s == 0:
-                for l in (0, 1):
-                    group_weights(l)
-                quantise_weights(0, 2)
                 acc = acc_pool.tile([P, MAX_UNITS * COUT], F32)
                 nc.tensor.matmul(out=acc[:, :DEGREES], lhsT=ones[:], rhs=pw_row[:], start=True, stop=True)
                 nc.vector.tensor_copy(out=pw[:], in_=acc[:, :DEGREES])
+            if s + 1 < len(rounds):
+                ordered_of[s + 1] = order_round(s + 1)
             if 1 <= s <= len(rounds):
                 quantised_of[s - 1] = quantise_round(s - 1, grouped_of[s - 1])
-            if s == 3:
-                for l in (2, 3):
-                    group_weights(l)
-                quantise_weights(2, 2)
-            if s + 2 < len(rounds):
-                ordered_of[s + 2] = order_round(s + 2)
             if s >= 2:
                 r = s - 2
                 tile, first_row, units = rounds[r]
-                if first_row == 0:
+                if tile not in out_of:
                     out_sb = out_pool.tile([P, ROWS * COUT], F32)
                     out_of[tile] = out_sb
                 codes, scales = quantised_of[r]
                 multiply_round(r, codes, scales, out_of[tile])
                 if tile == NODE_TILES - 1:
                     store_rows(tile, out_of[tile], first_row, units)
-                elif first_row + units == ROWS:
+                elif rounds[r + 1][0] != tile:
                     store_rows(tile, out_of[tile], 0, ROWS)
+            if s < len(rounds):
+                for l in new_degrees(rounds, s):
+                    group_weights(l)
+                    quantise_weights(l)

import concourse.mybir as mybir
from concourse.masks import make_identity

BF16 = mybir.dt.bfloat16
F32 = mybir.dt.float32
U32 = mybir.dt.uint32
U8 = mybir.dt.uint8
FP8X4 = mybir.dt.float8_e4m3fn_x4

NODES, ROWS, CIN, COUT, DEGREES = 512, 16, 1024, 128, 4
FLOPS = 2 * NODES * ROWS * CIN * COUT

P = 128
PACK = 4
K_PASS = P * PACK
PASSES = CIN // K_PASS
WORDS = CIN // 2
HALVES = PACK // 2

DEGREE_OF_ROW = [l for l in range(DEGREES) for i in range(2 * l + 1)]

NODE_TILES = NODES // P
MAX_UNITS = 4
HEAD = [(9, 1), (10, 2), (12, 2), (0, 1), (14, 2), (5, 4), (1, 4)]
BODY = [(0, 4), (4, 4), (8, 4), (12, 4)]
TAIL = [(0, 4), (4, 4), (8, 4), (12, 2), (14, 1), (15, 1)]


def all_rounds():
    rounds = []
    for tile in range(NODE_TILES):
        of_tile = HEAD if tile == 0 else TAIL if tile == NODE_TILES - 1 else BODY
        rounds.extend([(tile, first_row, units) for first_row, units in of_tile])
    return rounds


def new_degrees(rounds, r):
    tile, first_row, units = rounds[r]
    degrees = sorted(set(DEGREE_OF_ROW[first_row : first_row + units]))
    earlier = [DEGREE_OF_ROW[row] for t, first, count in rounds[:r] for row in range(first, first + count)]
    return [l for l in degrees if l not in earlier]


ORDERED = 2

X_BUFS = {1: 4, 2: 4, 4: 12}

def tile_linear_pa_t_kernel(tc, x, weights, path_weights, out):
    nc = tc.nc
    with (
        tc.tile_pool(name="const", bufs=1) as const,
        tc.tile_pool(name="x_pool", bufs=14) as x_pool,
        tc.tile_pool(name="ordered_pool", bufs=4) as ordered_pool,
        tc.tile_pool(name="grouped_pool", bufs=3) as grouped_pool,
        tc.tile_pool(name="quantised_pool", bufs=3) as quantised_pool,
        tc.tile_pool(name="out_pool", bufs=NODE_TILES) as out_pool,
        tc.psum_pool(name="xt_pool", bufs=6) as xt_pool,
        tc.psum_pool(name="acc_pool", bufs=2) as acc_pool,
        tc.manual_schedule(),
    ):
        rounds = all_rounds()

        def load_x_round(r):
            tile, first_row, units = rounds[r]
            x_sb = x_pool.tile([P, units * CIN], BF16, tag=f"x{units}", bufs=X_BUFS[units])
            nc.sync.dma_start(
                out=x_sb[:],
                in_=x[tile * P : (tile + 1) * P, first_row : first_row + units, :].rearrange("n m k -> n (m k)"),
            )
            return x_sb

        w_raw = const.tile([P, DEGREES * CIN], BF16)

        def load_weights(l):
            nc.sync.dma_start(
                out=w_raw[:, l * CIN : (l + 1) * CIN].rearrange("p (g tc) -> p g tc", tc=PACK * COUT),
                in_=weights[l].rearrange("(g p t) c -> p g (t c)", p=P, t=PACK),
            )

        x_tiles = []
        for r in range(len(rounds)):
            x_tiles.append(load_x_round(r))
            for l in new_degrees(rounds, r):
                load_weights(l)

        pw_row = const.tile([P, DEGREES], BF16)
        nc.gpsimd.memset(pw_row[:], 0.0)
        nc.scalar.dma_start(out=pw_row[0:1, :], in_=path_weights.rearrange("(o l) -> o l", o=1))

        ident = const.tile([P, P], F32)
        make_identity(nc, ident[:])
        ones = const.tile([P, P], BF16)
        nc.gpsimd.memset(ones[:], 1.0)
        pw = const.tile([P, DEGREES], F32)

        w_grouped = const.tile([P, DEGREES * CIN], BF16, align_bytes=64)
        w_codes = const.tile([P, DEGREES * PASSES * COUT], U32, align_bytes=64)
        w_scales = const.tile([P, DEGREES * PASSES * COUT], U8, align_bytes=64)

        def group_weights(l):
            nc.vector.tensor_copy(
                out=w_grouped[:, l * CIN : (l + 1) * CIN].rearrange("p (g c t) -> p g c t", c=COUT, t=PACK),
                in_=w_raw[:, l * CIN : (l + 1) * CIN].rearrange("p (g t c) -> p g c t", c=COUT, t=PACK),
            )

        def quantise_weights(l):
            words = slice(l * PASSES * COUT, (l + 1) * PASSES * COUT)
            nc.vector.quantize_mx(
                out=w_codes[:, words].bitcast(FP8X4),
                scales=w_scales[:, words],
                in_=w_grouped[:, l * CIN : (l + 1) * CIN],
            )

        def order_round(r):
            if rounds[r][2] < MAX_UNITS:
                return None
            x_words = x_tiles[r][:].bitcast(F32)
            ordered = ordered_pool.tile([P, ORDERED * CIN], BF16)
            nc.vector.tensor_copy(
                out=ordered[:].bitcast(F32).rearrange("p (b u w) -> p b u w", u=HALVES, w=P),
                in_=x_words[:, (MAX_UNITS - ORDERED) * WORDS :].rearrange("p (b w u) -> p b u w", w=P, u=HALVES),
            )
            return ordered

        def transpose_round(r, ordered):
            units = rounds[r][2]
            x_words = x_tiles[r][:].bitcast(F32)
            grouped = grouped_pool.tile([P, units * CIN], BF16, tag="grouped", align_bytes=64)
            for unit in range(units):
                xt = xt_pool.tile([P, WORDS], F32)
                for j in range(WORDS // P):
                    g, u = divmod(j, HALVES)
                    if ordered is None or unit < MAX_UNITS - ORDERED:
                        first = unit * WORDS + g * HALVES * P + u
                        words = x_words[:, first : first + HALVES * (P - 1) + 1 : HALVES]
                    else:
                        first = (unit - (MAX_UNITS - ORDERED)) * WORDS + j * P
                        words = ordered[:].bitcast(F32)[:, first : first + P]
                    nc.tensor.transpose(xt[:, j * P : (j + 1) * P], words, ident[:])
                nc.scalar.copy(
                    out=grouped[:, unit * CIN : (unit + 1) * CIN]
                    .bitcast(F32)
                    .rearrange("p (g n u) -> p g n u", g=PASSES, u=HALVES),
                    in_=xt[:].rearrange("p (g u n) -> p g n u", g=PASSES, u=HALVES),
                )
            return grouped

        def quantise_round(r, grouped):
            words = rounds[r][2] * PASSES * P
            codes = quantised_pool.tile([P, words], U32, tag="codes", align_bytes=64)
            scales = quantised_pool.tile([P, words], U8, tag="scales", align_bytes=64)
            nc.vector.quantize_mx(out=codes[:].bitcast(FP8X4), scales=scales[:], in_=grouped[:])
            return codes, scales

        def multiply_round(r, codes, scales, out_sb):
            first_row, units = rounds[r][1:]
            acc = acc_pool.tile([P, MAX_UNITS * COUT], F32)
            for unit in range(units):
                l = DEGREE_OF_ROW[first_row + unit]
                for g in range(PASSES):
                    x_cols = slice((unit * PASSES + g) * P, (unit * PASSES + g + 1) * P)
                    w_cols = slice((l * PASSES + g) * COUT, (l * PASSES + g + 1) * COUT)
                    nc.tensor.matmul_mx(
                        out=acc[:, unit * COUT : (unit + 1) * COUT],
                        lhsT=codes[:, x_cols].bitcast(FP8X4),
                        lhsT_scale=scales[:, x_cols],
                        rhs=w_codes[:, w_cols].bitcast(FP8X4),
                        rhs_scale=w_scales[:, w_cols],
                        start=(g == 0),
                        stop=(g == PASSES - 1),
                    )
            for l in range(DEGREES):
                units_of_l = [unit for unit in range(units) if DEGREE_OF_ROW[first_row + unit] == l]
                if not units_of_l:
                    continue
                first, count = units_of_l[0], len(units_of_l)
                src = acc[:, first * COUT : (first + count) * COUT]
                dst = out_sb[:, (first_row + first) * COUT : (first_row + first + count) * COUT]
                if r % 2 == 0:
                    nc.vector.tensor_scalar(
                        out=dst, in0=src, scalar1=pw[:, l : l + 1], scalar2=None, op0=mybir.AluOpType.mult
                    )
                else:
                    nc.scalar.activation(
                        out=dst, in_=src, func=mybir.ActivationFunctionType.Copy, scale=pw[:, l : l + 1]
                    )

        def store_rows(tile, out_sb, first_row, rows):
            nc.sync.dma_start(
                out=out[tile * P : (tile + 1) * P, first_row : first_row + rows, :].rearrange("n m c -> n (m c)"),
                in_=out_sb[:, first_row * COUT : (first_row + rows) * COUT],
            )

        ordered_of = {}
        grouped_of = {}
        quantised_of = {}
        out_of = {}
        ordered_of[0] = order_round(0)
        for s in range(len(rounds) + 2):
            if s < len(rounds):
                grouped_of[s] = transpose_round(s, ordered_of[s])
            if s == 0:
                acc = acc_pool.tile([P, MAX_UNITS * COUT], F32)
                nc.tensor.matmul(out=acc[:, :DEGREES], lhsT=ones[:], rhs=pw_row[:], start=True, stop=True)
                nc.vector.tensor_copy(out=pw[:], in_=acc[:, :DEGREES])
            if s + 1 < len(rounds):
                ordered_of[s + 1] = order_round(s + 1)
            if 1 <= s <= len(rounds):
                quantised_of[s - 1] = quantise_round(s - 1, grouped_of[s - 1])
            if s >= 2:
                r = s - 2
                tile, first_row, units = rounds[r]
                if tile not in out_of:
                    out_sb = out_pool.tile([P, ROWS * COUT], F32)
                    out_of[tile] = out_sb
                codes, scales = quantised_of[r]
                multiply_round(r, codes, scales, out_of[tile])
                if tile == NODE_TILES - 1:
                    store_rows(tile, out_of[tile], first_row, units)
                elif rounds[r + 1][0] != tile:
                    store_rows(tile, out_of[tile], 0, ROWS)
            if s < len(rounds):
                for l in new_degrees(rounds, s):
                    group_weights(l)
                    quantise_weights(l)
